import numpy as np
import ml_dtypes


BF16 = ml_dtypes.bfloat16


def bf(x):
    return np.asarray(x, np.float32).astype(BF16)


def f64(x):
    return np.asarray(x).astype(np.float64)


E2M1 = np.array([0.0, 0.5, 1.0, 1.5, 2.0, 3.0, 4.0, 6.0, -0.0, -0.5, -1.0, -1.5, -2.0, -3.0, -4.0, -6.0])


def pack_weight(w, fmt):
    k, n = w.shape
    w = f64(bf(w)).reshape(k // 32, 32, n)
    amax = np.abs(w).max(1)
    if fmt == "e4m3":
        byte = np.frexp(amax)[1] - 1 + 127 - 7
    else:
        mant, ex = np.frexp(amax / 6.0)
        byte = np.where(mant > 0.5, ex, ex - 1) + 127
    byte = np.clip(np.where(amax > 0, byte, 1), 1, 254)
    scaled = (w * np.exp2(127.0 - byte)[:, None, :]).reshape(k, n).astype(np.float32)
    by_word = np.ascontiguousarray(scaled.reshape(k // 512, 128, 4, n).transpose(0, 1, 3, 2))
    if fmt == "e4m3":
        words = by_word.astype(ml_dtypes.float8_e4m3fn).view(np.uint8)
    else:
        c = by_word.astype(ml_dtypes.float4_e2m1fn).view(np.uint8) & 0xF
        words = c[..., 0::2] | (c[..., 1::2] << 4)
    return np.ascontiguousarray(words), np.ascontiguousarray(byte.astype(np.uint8).reshape(k // 512, 16, n))


def unpack_weight(words, scales, fmt):
    g, p, n, _ = words.shape
    if fmt == "e4m3":
        vals = np.ascontiguousarray(words).view(ml_dtypes.float8_e4m3fn).astype(np.float64)
    else:
        nib = np.empty((g, p, n, 4), np.uint8)
        nib[..., 0::2] = words & 0xF
        nib[..., 1::2] = words >> 4
        vals = E2M1[nib]
    vals = vals * np.repeat(np.exp2(scales.astype(np.float64) - 127.0), 8, axis=1)[..., None]
    return vals.transpose(0, 1, 3, 2).reshape(g * 512, n)

def pack4(w):
    words, scales = pack_weight(w, "e2m1")
    return words.reshape(words.shape[0], 128, -1), scales


def unpack4(words, scales):
    return unpack_weight(words.reshape(words.shape[0], 128, -1, 2), scales, "e2m1")


def kspread(k):
    return np.exp2(np.repeat(np.random.randint(-6, 7, k // 32), 32).astype(np.float64))


L, D, HQ, HKV, HD, WIN, ROPE_BASE = 512, 3072, 16, 4, 128, 256, 1024
HALF = HD // 2
QUART = HALF // 2
NQ = HQ * HD
NKV = HKV * HD


def rope_tables():
    freqs = (1.0 / ROPE_BASE) ** np.linspace(0.0, 1.0, num=QUART)
    freqs = np.concatenate([freqs, np.zeros(QUART)])
    theta = np.arange(L, dtype=np.float64)[:, None] * freqs[None, :]
    return np.cos(theta)[:, None, :], np.sin(theta)[:, None, :]


def rotate(u, cos, sin):
    u1, u2 = u[..., :HALF], u[..., HALF:]
    return np.concatenate([u1 * cos + u2 * sin, -u1 * sin + u2 * cos], axis=-1)


def setup_inputs():
    s = kspread(D)
    x = np.random.standard_normal((L, D)) * s
    x_words, x_scales = pack4(np.ascontiguousarray(x.reshape(L, D).T))
    words, scales = pack4(np.random.standard_normal((D, NQ + NKV + NKV)) * 1.25 / np.sqrt(D) / s[:, None])
    return {"x_words": x_words, "x_scales": x_scales, "Wqkv_words": words, "Wqkv_scales": scales}


def reference(x_words, x_scales, Wqkv_words, Wqkv_scales):
    proj = unpack4(x_words, x_scales).T @ unpack4(Wqkv_words, Wqkv_scales)
    q = proj[:, :NQ].reshape(L, HQ, HD)
    k = proj[:, NQ:NQ + NKV].reshape(L, HKV, HD)
    v = proj[:, NQ + NKV:].reshape(L, HKV, HD)
    cos, sin = rope_tables()
    return rotate(q, cos, sin), rotate(k, cos, sin), v

@@ -1,0 +1,205 @@
+import math
+from contextlib import ExitStack
+
+import concourse.mybir as mybir
+
+L, D, N_OUT = 512, 3072, 3072
+FLOPS = 2 * L * D * N_OUT
+
+P = 128
+PASSES = D // 512
+CHUNK = 512
+HEAD = 128
+ROT = 32
+BLOCKS = L // P
+ROPE_BASE = 1024
+WARMUPS = 10
+
+F32 = mybir.dt.float32
+BF16 = mybir.dt.bfloat16
+I32 = mybir.dt.int32
+U8 = mybir.dt.uint8
+FP4X4 = mybir.dt.float4_e2m1fn_x4
+ALU = mybir.AluOpType
+ACT = mybir.ActivationFunctionType
+
+
+def tile_groupedqueryattention_pa_kernel(tc, x_words, x_scales, w_words, w_scales, q_out, k_out, v_out):
+    nc = tc.nc
+    outs = [(q_out.rearrange("l h d -> l (h d)"), c * CHUNK) for c in range(4)]
+    outs.append((k_out.rearrange("l h d -> l (h d)"), 0))
+    outs.append((v_out.rearrange("l h d -> l (h d)"), 0))
+
+    with ExitStack() as ctx:
+        keep = ctx.enter_context(tc.tile_pool(name="keep", bufs=1))
+        work = ctx.enter_context(tc.tile_pool(name="work", bufs=4))
+        psum = ctx.enter_context(tc.psum_pool(name="psum", bufs=1))
+        ctx.enter_context(tc.manual_schedule())
+
+        xc = keep.tile([P, PASSES, 2 * L], U8, name="xc", align_bytes=256)
+        xs = keep.tile([P, PASSES, L], U8, name="xs", align_bytes=256)
+        wc = []
+        ws = []
+        for s in range(3):
+            wc.append(keep.tile([P, PASSES, 4 * CHUNK], U8, name="wc%d" % s, align_bytes=256))
+            ws.append(keep.tile([P, PASSES, 2 * CHUNK], U8, name="ws%d" % s, align_bytes=256))
+        zeros = keep.tile([P, CHUNK], BF16, name="zeros", align_bytes=256)
+        pos = keep.tile([P, BLOCKS], I32, name="pos")
+        turns = keep.tile([P, BLOCKS, ROT], F32, name="turns")
+        whole = keep.tile([P, BLOCKS, ROT], I32, name="whole")
+        frac = keep.tile([P, BLOCKS, ROT], F32, name="frac")
+        half_sin = keep.tile([P, BLOCKS, ROT], F32, name="half_sin")
+        cos_t = keep.tile([P, BLOCKS, ROT], F32, name="cos_t")
+        sin_t = keep.tile([P, BLOCKS, 2, ROT], F32, name="sin_t")
+
+        nc.vector.memset(zeros[:], 0.0)
+        nc.vector.memset(xs[:, 0:2, :].bitcast(I32), 0)
+        nc.vector.memset(ws[0][:, 0:1, :].bitcast(I32), 0)
+        nc.gpsimd.memset(ws[0][:, 1:2, :].bitcast(I32), 0)
+        nc.gpsimd.iota(pos[:], pattern=[[P, BLOCKS]], base=0, channel_multiplier=1)
+        nc.vector.memset(xs[:, 2:6, :].bitcast(I32), 0)
+        nc.vector.memset(ws[0][:, 2:6, :].bitcast(I32), 0)
+        nc.gpsimd.memset(ws[1][:].bitcast(I32), 0)
+        nc.gpsimd.memset(ws[2][:].bitcast(I32), 0)
+
+        def load_x_codes(g0, g1):
+            nc.sync.dma_start(
+                out=xc[:, g0:g1, :].bitcast(I32),
+                in_=x_words[g0:g1].rearrange("g p n -> p g n").bitcast(I32),
+            )
+
+        def load_w_codes(s, g0, g1, a, b):
+            base = s * 4 * CHUNK
+            nc.sync.dma_start(
+                out=wc[s][:, g0:g1, a:b].bitcast(I32),
+                in_=w_words[g0:g1, :, base + a : base + b].rearrange("g p n -> p g n").bitcast(I32),
+            )
+
+        def load_x_scales(g0, g1):
+            for q in range(4):
+                nc.sync.dma_start(
+                    out=xs[32 * q : 32 * q + 4, g0:g1, :].bitcast(I32),
+                    in_=x_scales[g0:g1, 4 * q : 4 * q + 4, :].rearrange("g r n -> r g n").bitcast(I32),
+                )
+
+        def load_w_scales(s, g0, g1):
+            base = s * 2 * CHUNK
+            for q in range(4):
+                nc.sync.dma_start(
+                    out=ws[s][32 * q : 32 * q + 4, g0:g1, :].bitcast(I32),
+                    in_=w_scales[g0:g1, 4 * q : 4 * q + 4, base : base + 2 * CHUNK]
+                    .rearrange("g r n -> r g n")
+                    .bitcast(I32),
+                )
+
+        load_x_codes(0, 1)
+        load_w_codes(0, 0, 1, 0, 2 * CHUNK)
+        load_x_scales(0, 2)
+        load_w_scales(0, 0, 2)
+        load_w_codes(0, 0, 1, 2 * CHUNK, 4 * CHUNK)
+        load_x_codes(1, 2)
+        load_w_codes(0, 1, 2, 0, 4 * CHUNK)
+        load_x_scales(2, 6)
+        load_w_scales(0, 2, 6)
+        load_x_codes(2, 4)
+        load_w_codes(0, 2, 4, 0, 4 * CHUNK)
+        load_x_codes(4, 6)
+        load_w_codes(0, 4, 6, 0, 4 * CHUNK)
+        for s in (1, 2):
+            load_w_scales(s, 0, 6)
+            for g in range(0, 6, 2):
+                load_w_codes(s, g, g + 2, 0, 4 * CHUNK)
+
+        nc.vector.tensor_scalar(out=turns[:, :, 0], in0=pos[:], scalar1=0.5 / math.pi, scalar2=None, op0=ALU.mult)
+        ratio = ROPE_BASE ** (-1.0 / (ROT - 1))
+        for w in (1, 2, 4, 8, 16):
+            nc.vector.tensor_scalar(
+                out=turns[:, :, w : 2 * w], in0=turns[:, :, 0:w], scalar1=ratio**w, scalar2=None, op0=ALU.mult
+            )
+        nc.vector.tensor_copy(out=whole[:], in_=turns[:])
+        nc.vector.tensor_tensor(out=frac[:], in0=turns[:], in1=whole[:], op=ALU.subtract)
+        nc.scalar.activation(out=sin_t[:, :, 0, :], in_=frac[:], func=ACT.Sin, scale=-2.0 * math.pi)
+        nc.scalar.activation(out=sin_t[:, :, 1, :], in_=frac[:], func=ACT.Sin, scale=2.0 * math.pi)
+        nc.scalar.activation(out=half_sin[:], in_=frac[:], func=ACT.Sin, scale=math.pi)
+        nc.vector.scalar_tensor_tensor(
+            out=cos_t[:], in0=half_sin[:], scalar=-2.0, in1=half_sin[:], op0=ALU.mult, op1=ALU.mult
+        )
+        nc.vector.tensor_scalar(out=cos_t[:], in0=cos_t[:], scalar1=1.0, scalar2=None, op0=ALU.add)
+
+        def bank(i):
+            return psum.tile([P, CHUNK], F32, name="bank%d" % (i % 8), tag="bank%d" % (i % 8))
+
+        warm = bank(7)
+        for i in range(WARMUPS):
+            nc.tensor.matmul(out=warm[:], lhsT=zeros[:, 0:P], rhs=zeros[:], start=True, stop=True)
+
+        def mm(acc, g, b, c, a, n):
+            s, o = c // 2, (c % 2) * CHUNK + a
+            nc.tensor.matmul_mx(
+                out=acc[:, a : a + n],
+                lhsT=xc[:, g, 2 * P * b : 2 * P * (b + 1)].bitcast(FP4X4),
+                lhsT_scale=xs[:, g, P * b : P * (b + 1)],
+                rhs=wc[s][:, g, 2 * o : 2 * (o + n)].bitcast(FP4X4),
+                rhs_scale=ws[s][:, g, o : o + n],
+                start=(g == 0),
+                stop=(g == PASSES - 1),
+            )
+
+        def store(res, b, c, a, n):
+            dst, o = outs[c]
+            nc.sync.dma_start(out=dst[P * b : P * (b + 1), o + a : o + a + n], in_=res[:, a : a + n])
+
+        def rope(acc, b, c):
+            res = work.tile([P, CHUNK], F32, name="res", align_bytes=256)
+            t_cos = work.tile([P, 8, ROT], F32, name="t_cos", align_bytes=256)
+            t_sin = work.tile([P, 4, 2, ROT], F32, name="t_sin", align_bytes=256)
+            src = acc[:].rearrange("p (h s r j) -> p h s r j", h=4, s=2, r=2)
+            src8 = acc[:].rearrange("p (h r j) -> p h r j", h=8, r=2)
+            dst = res[:].rearrange("p (h s r j) -> p h s r j", h=4, s=2, r=2)
+            dst8 = res[:].rearrange("p (h r j) -> p h r j", h=8, r=2)
+            nc.vector.tensor_tensor(
+                out=t_cos[:],
+                in0=src8[:, :, 0, :],
+                in1=cos_t[:, b, :].unsqueeze(1).to_broadcast([P, 8, ROT]),
+                op=ALU.mult,
+            )
+            nc.vector.tensor_tensor(
+                out=t_sin[:],
+                in0=src[:, :, :, 0, :],
+                in1=sin_t[:, b, :, :].unsqueeze(1).to_broadcast([P, 4, 2, ROT]),
+                op=ALU.mult,
+            )
+            nc.scalar.copy(out=dst8[:, :, 1, :], in_=src8[:, :, 1, :])
+            nc.vector.tensor_tensor(
+                out=dst[:, :, :, 0, :],
+                in0=t_cos[:].rearrange("p (h s) j -> p h s j", s=2),
+                in1=t_sin[:, :, ::-1, :],
+                op=ALU.add,
+            )
+            store(res, b, c, 0, CHUNK)
+
+        accs = [bank(i) for i in range(8)]
+        for g in range(PASSES):
+            for i in range(8):
+                mm(accs[i], g, i % 4, i // 4, 0, CHUNK)
+        for i in range(8):
+            rope(accs[i], i % 4, i // 4)
+
+        i = 0
+        for c in (2, 3, 4, 5):
+            for b in range(4):
+                last = c == 5 and b == 3
+                for a, n in [(0, 256), (256, 128), (384, 128)] if last else [(0, CHUNK)]:
+                    acc = bank(i)
+                    i += 1
+                    for g in range(PASSES):
+                        mm(acc, g, b, c, a, n)
+                    if c < 5:
+                        rope(acc, b, c)
+                    else:
+                        res = work.tile([P, CHUNK], F32, name="res", align_bytes=256)
+                        if a == 384:
+                            nc.vector.tensor_copy(out=res[:, a : a + n], in_=acc[:, a : a + n])
+                        else:
+                            nc.scalar.copy(out=res[:, a : a + n], in_=acc[:, a : a + n])
+                        store(res, b, c, a, n)

@@ -40,9 +40,11 @@ def tile_groupedqueryattention_pa_kernel(tc, x_words, x_scales, w_words, w_scale
         xs = keep.tile([P, PASSES, L], U8, name="xs", align_bytes=256)
         wc = []
         ws = []
-        for s in range(3):
-            wc.append(keep.tile([P, PASSES, 4 * CHUNK], U8, name="wc%d" % s, align_bytes=256))
-            ws.append(keep.tile([P, PASSES, 2 * CHUNK], U8, name="ws%d" % s, align_bytes=256))
+        first = [0, 1024, 1536, 2048, 2560]
+        width = [1024, 512, 512, 512, 512]
+        for s in range(5):
+            wc.append(keep.tile([P, PASSES, 2 * width[s]], U8, name="wc%d" % s, align_bytes=256))
+            ws.append(keep.tile([P, PASSES, width[s]], U8, name="ws%d" % s, align_bytes=256))
         zeros = keep.tile([P, CHUNK], BF16, name="zeros", align_bytes=256)
         pos = keep.tile([P, BLOCKS], I32, name="pos")
         turns = keep.tile([P, BLOCKS, ROT], F32, name="turns")
@@ -59,8 +61,8 @@ def tile_groupedqueryattention_pa_kernel(tc, x_words, x_scales, w_words, w_scale
         nc.gpsimd.iota(pos[:], pattern=[[P, BLOCKS]], base=0, channel_multiplier=1)
         nc.vector.memset(xs[:, 2:6, :].bitcast(I32), 0)
         nc.vector.memset(ws[0][:, 2:6, :].bitcast(I32), 0)
-        nc.gpsimd.memset(ws[1][:].bitcast(I32), 0)
-        nc.gpsimd.memset(ws[2][:].bitcast(I32), 0)
+        for s in range(1, 5):
+            nc.gpsimd.memset(ws[s][:].bitcast(I32), 0)
 
         def load_x_codes(g0, g1):
             nc.sync.dma_start(
@@ -69,25 +71,25 @@ def tile_groupedqueryattention_pa_kernel(tc, x_words, x_scales, w_words, w_scale
             )
 
         def load_w_codes(s, g0, g1, a, b):
-            base = s * 4 * CHUNK
+            base = 2 * first[s]
             nc.sync.dma_start(
                 out=wc[s][:, g0:g1, a:b].bitcast(I32),
                 in_=w_words[g0:g1, :, base + a : base + b].rearrange("g p n -> p g n").bitcast(I32),
             )
 
         def load_x_scales(g0, g1):
-            for q in range(4):
+            for q in (0, 2, 1, 3):
                 nc.sync.dma_start(
                     out=xs[32 * q : 32 * q + 4, g0:g1, :].bitcast(I32),
                     in_=x_scales[g0:g1, 4 * q : 4 * q + 4, :].rearrange("g r n -> r g n").bitcast(I32),
                 )
 
         def load_w_scales(s, g0, g1):
-            base = s * 2 * CHUNK
-            for q in range(4):
+            base = first[s]
+            for q in (0, 2, 1, 3):
                 nc.sync.dma_start(
                     out=ws[s][32 * q : 32 * q + 4, g0:g1, :].bitcast(I32),
-                    in_=w_scales[g0:g1, 4 * q : 4 * q + 4, base : base + 2 * CHUNK]
+                    in_=w_scales[g0:g1, 4 * q : 4 * q + 4, base : base + width[s]]
                     .rearrange("g r n -> r g n")
                     .bitcast(I32),
                 )
@@ -100,15 +102,17 @@ def tile_groupedqueryattention_pa_kernel(tc, x_words, x_scales, w_words, w_scale
         load_x_codes(1, 2)
         load_w_codes(0, 1, 2, 0, 4 * CHUNK)
         load_x_scales(2, 6)
-        load_w_scales(0, 2, 6)
+        load_w_scales(0, 2, 4)
         load_x_codes(2, 4)
-        load_w_codes(0, 2, 4, 0, 4 * CHUNK)
+        load_w_codes(0, 2, 3, 0, 4 * CHUNK)
+        load_w_codes(0, 3, 4, 0, 4 * CHUNK)
+        load_w_scales(0, 4, 6)
         load_x_codes(4, 6)
         load_w_codes(0, 4, 6, 0, 4 * CHUNK)
-        for s in (1, 2):
+        for s in range(1, 5):
             load_w_scales(s, 0, 6)
-            for g in range(0, 6, 2):
-                load_w_codes(s, g, g + 2, 0, 4 * CHUNK)
+            load_w_codes(s, 0, 3, 0, 2 * CHUNK)
+            load_w_codes(s, 3, 6, 0, 2 * CHUNK)
 
         nc.vector.tensor_scalar(out=turns[:, :, 0], in0=pos[:], scalar1=0.5 / math.pi, scalar2=None, op0=ALU.mult)
         ratio = ROPE_BASE ** (-1.0 / (ROT - 1))
@@ -134,7 +138,8 @@ def tile_groupedqueryattention_pa_kernel(tc, x_words, x_scales, w_words, w_scale
             nc.tensor.matmul(out=warm[:], lhsT=zeros[:, 0:P], rhs=zeros[:], start=True, stop=True)
 
         def mm(acc, g, b, c, a, n):
-            s, o = c // 2, (c % 2) * CHUNK + a
+            s = max(c - 1, 0)
+            o = c * CHUNK - first[s] + a
             nc.tensor.matmul_mx(
                 out=acc[:, a : a + n],
                 lhsT=xc[:, g, 2 * P * b : 2 * P * (b + 1)].bitcast(FP4X4),
@@ -150,7 +155,7 @@ def tile_groupedqueryattention_pa_kernel(tc, x_words, x_scales, w_words, w_scale
             nc.sync.dma_start(out=dst[P * b : P * (b + 1), o + a : o + a + n], in_=res[:, a : a + n])
 
         def rope(acc, b, c):
-            res = work.tile([P, CHUNK], F32, name="res", align_bytes=256)
+            res = work.tile([P, CHUNK], F32, name="res", bufs=24, align_bytes=256)
             t_cos = work.tile([P, 8, ROT], F32, name="t_cos", align_bytes=256)
             t_sin = work.tile([P, 4, 2, ROT], F32, name="t_sin", align_bytes=256)
             src = acc[:].rearrange("p (h s r j) -> p h s r j", h=4, s=2, r=2)
@@ -197,7 +202,7 @@ def tile_groupedqueryattention_pa_kernel(tc, x_words, x_scales, w_words, w_scale
                     if c < 5:
                         rope(acc, b, c)
                     else:
-                        res = work.tile([P, CHUNK], F32, name="res", align_bytes=256)
+                        res = work.tile([P, CHUNK], F32, name="res", bufs=24, align_bytes=256)
                         if a == 384:
                             nc.vector.tensor_copy(out=res[:, a : a + n], in_=acc[:, a : a + n])
                         else:

@@ -13,7 +13,7 @@ HEAD = 128
 ROT = 32
 BLOCKS = L // P
 ROPE_BASE = 1024
-WARMUPS = 10
+WARMUPS = 8
 
 F32 = mybir.dt.float32
 BF16 = mybir.dt.bfloat16
@@ -54,20 +54,19 @@ def tile_groupedqueryattention_pa_kernel(tc, x_words, x_scales, w_words, w_scale
         cos_t = keep.tile([P, BLOCKS, ROT], F32, name="cos_t")
         sin_t = keep.tile([P, BLOCKS, 2, ROT], F32, name="sin_t")
 
-        nc.vector.memset(zeros[:], 0.0)
+        nc.gpsimd.memset(zeros[:], 0.0)
         nc.vector.memset(xs[:, 0:2, :].bitcast(I32), 0)
-        nc.vector.memset(ws[0][:, 0:1, :].bitcast(I32), 0)
-        nc.gpsimd.memset(ws[0][:, 1:2, :].bitcast(I32), 0)
+        nc.vector.memset(ws[0][:, 0:2, :].bitcast(I32), 0)
         nc.gpsimd.iota(pos[:], pattern=[[P, BLOCKS]], base=0, channel_multiplier=1)
         nc.vector.memset(xs[:, 2:6, :].bitcast(I32), 0)
         nc.vector.memset(ws[0][:, 2:6, :].bitcast(I32), 0)
         for s in range(1, 5):
             nc.gpsimd.memset(ws[s][:].bitcast(I32), 0)
 
-        def load_x_codes(g0, g1):
+        def load_x_codes(g0, g1, a=0, b=2 * L):
             nc.sync.dma_start(
-                out=xc[:, g0:g1, :].bitcast(I32),
-                in_=x_words[g0:g1].rearrange("g p n -> p g n").bitcast(I32),
+                out=xc[:, g0:g1, a:b].bitcast(I32),
+                in_=x_words[g0:g1, :, a:b].rearrange("g p n -> p g n").bitcast(I32),
             )
 
         def load_w_codes(s, g0, g1, a, b):
@@ -94,10 +93,11 @@ def tile_groupedqueryattention_pa_kernel(tc, x_words, x_scales, w_words, w_scale
                     .bitcast(I32),
                 )
 
-        load_x_codes(0, 1)
+        load_x_codes(0, 1, 0, L)
         load_w_codes(0, 0, 1, 0, 2 * CHUNK)
         load_x_scales(0, 2)
         load_w_scales(0, 0, 2)
+        load_x_codes(0, 1, L, 2 * L)
         load_w_codes(0, 0, 1, 2 * CHUNK, 4 * CHUNK)
         load_x_codes(1, 2)
         load_w_codes(0, 1, 2, 0, 4 * CHUNK)
@@ -150,9 +150,9 @@ def tile_groupedqueryattention_pa_kernel(tc, x_words, x_scales, w_words, w_scale
                 stop=(g == PASSES - 1),
             )
 
-        def store(res, b, c, a, n):
+        def store(res, b, c, a, n, queue):
             dst, o = outs[c]
-            nc.sync.dma_start(out=dst[P * b : P * (b + 1), o + a : o + a + n], in_=res[:, a : a + n])
+            queue.dma_start(out=dst[P * b : P * (b + 1), o + a : o + a + n], in_=res[:, a : a + n])
 
         def rope(acc, b, c):
             res = work.tile([P, CHUNK], F32, name="res", bufs=24, align_bytes=256)
@@ -181,7 +181,7 @@ def tile_groupedqueryattention_pa_kernel(tc, x_words, x_scales, w_words, w_scale
                 in1=t_sin[:, :, ::-1, :],
                 op=ALU.add,
             )
-            store(res, b, c, 0, CHUNK)
+            store(res, b, c, 0, CHUNK, nc.sync)
 
         accs = [bank(i) for i in range(8)]
         for g in range(PASSES):
@@ -203,8 +203,8 @@ def tile_groupedqueryattention_pa_kernel(tc, x_words, x_scales, w_words, w_scale
                         rope(acc, b, c)
                     else:
                         res = work.tile([P, CHUNK], F32, name="res", bufs=24, align_bytes=256)
-                        if a == 384:
+                        if a == 256:
                             nc.vector.tensor_copy(out=res[:, a : a + n], in_=acc[:, a : a + n])
                         else:
                             nc.scalar.copy(out=res[:, a : a + n], in_=acc[:, a : a + n])
-                        store(res, b, c, a, n)
+                        store(res, b, c, a, n, nc.scalar if a == 384 else nc.sync)

import math
from contextlib import ExitStack

import concourse.mybir as mybir

L, D, N_OUT = 512, 3072, 3072
FLOPS = 2 * L * D * N_OUT

P = 128
PASSES = D // 512
CHUNK = 512
HEAD = 128
ROT = 32
BLOCKS = L // P
ROPE_BASE = 1024
WARMUPS = 8

F32 = mybir.dt.float32
BF16 = mybir.dt.bfloat16
I32 = mybir.dt.int32
U8 = mybir.dt.uint8
FP4X4 = mybir.dt.float4_e2m1fn_x4
ALU = mybir.AluOpType
ACT = mybir.ActivationFunctionType


def tile_groupedqueryattention_pa_kernel(tc, x_words, x_scales, w_words, w_scales, q_out, k_out, v_out):
    nc = tc.nc
    outs = [(q_out.rearrange("l h d -> l (h d)"), c * CHUNK) for c in range(4)]
    outs.append((k_out.rearrange("l h d -> l (h d)"), 0))
    outs.append((v_out.rearrange("l h d -> l (h d)"), 0))

    with ExitStack() as ctx:
        keep = ctx.enter_context(tc.tile_pool(name="keep", bufs=1))
        work = ctx.enter_context(tc.tile_pool(name="work", bufs=4))
        psum = ctx.enter_context(tc.psum_pool(name="psum", bufs=1))
        ctx.enter_context(tc.manual_schedule())

        xc = keep.tile([P, PASSES, 2 * L], U8, name="xc", align_bytes=256)
        xs = keep.tile([P, PASSES, L], U8, name="xs", align_bytes=256)
        wc = []
        ws = []
        first = [0, 1024, 1536, 2048, 2560]
        width = [1024, 512, 512, 512, 512]
        for s in range(5):
            wc.append(keep.tile([P, PASSES, 2 * width[s]], U8, name="wc%d" % s, align_bytes=256))
            ws.append(keep.tile([P, PASSES, width[s]], U8, name="ws%d" % s, align_bytes=256))
        zeros = keep.tile([P, CHUNK], BF16, name="zeros", align_bytes=256)
        pos = keep.tile([P, BLOCKS], I32, name="pos")
        turns = keep.tile([P, BLOCKS, ROT], F32, name="turns")
        whole = keep.tile([P, BLOCKS, ROT], I32, name="whole")
        frac = keep.tile([P, BLOCKS, ROT], F32, name="frac")
        half_sin = keep.tile([P, BLOCKS, ROT], F32, name="half_sin")
        cos_t = keep.tile([P, BLOCKS, ROT], F32, name="cos_t")
        sin_t = keep.tile([P, BLOCKS, 2, ROT], F32, name="sin_t")

        nc.gpsimd.memset(zeros[:], 0.0)
        nc.vector.memset(xs[:, 0:2, :].bitcast(I32), 0)
        nc.vector.memset(ws[0][:, 0:2, :].bitcast(I32), 0)
        nc.gpsimd.iota(pos[:], pattern=[[P, BLOCKS]], base=0, channel_multiplier=1)
        nc.vector.memset(xs[:, 2:6, :].bitcast(I32), 0)
        nc.vector.memset(ws[0][:, 2:6, :].bitcast(I32), 0)
        for s in range(1, 5):
            nc.gpsimd.memset(ws[s][:].bitcast(I32), 0)

        def load_x_codes(g0, g1, a=0, b=2 * L):
            nc.sync.dma_start(
                out=xc[:, g0:g1, a:b].bitcast(I32),
                in_=x_words[g0:g1, :, a:b].rearrange("g p n -> p g n").bitcast(I32),
            )

        def load_w_codes(s, g0, g1, a, b):
            base = 2 * first[s]
            nc.sync.dma_start(
                out=wc[s][:, g0:g1, a:b].bitcast(I32),
                in_=w_words[g0:g1, :, base + a : base + b].rearrange("g p n -> p g n").bitcast(I32),
            )

        def load_x_scales(g0, g1):
            for q in (0, 2, 1, 3):
                nc.sync.dma_start(
                    out=xs[32 * q : 32 * q + 4, g0:g1, :].bitcast(I32),
                    in_=x_scales[g0:g1, 4 * q : 4 * q + 4, :].rearrange("g r n -> r g n").bitcast(I32),
                )

        def load_w_scales(s, g0, g1):
            base = first[s]
            for q in (0, 2, 1, 3):
                nc.sync.dma_start(
                    out=ws[s][32 * q : 32 * q + 4, g0:g1, :].bitcast(I32),
                    in_=w_scales[g0:g1, 4 * q : 4 * q + 4, base : base + width[s]]
                    .rearrange("g r n -> r g n")
                    .bitcast(I32),
                )

        load_x_codes(0, 1, 0, L)
        load_w_codes(0, 0, 1, 0, 2 * CHUNK)
        load_x_scales(0, 2)
        load_w_scales(0, 0, 2)
        load_x_codes(0, 1, L, 2 * L)
        load_w_codes(0, 0, 1, 2 * CHUNK, 4 * CHUNK)
        load_x_codes(1, 2)
        load_w_codes(0, 1, 2, 0, 4 * CHUNK)
        load_x_scales(2, 6)
        load_w_scales(0, 2, 4)
        load_x_codes(2, 4)
        load_w_codes(0, 2, 3, 0, 4 * CHUNK)
        load_w_codes(0, 3, 4, 0, 4 * CHUNK)
        load_w_scales(0, 4, 6)
        load_x_codes(4, 6)
        load_w_codes(0, 4, 6, 0, 4 * CHUNK)
        for s in range(1, 5):
            load_w_scales(s, 0, 6)
            load_w_codes(s, 0, 3, 0, 2 * CHUNK)
            load_w_codes(s, 3, 6, 0, 2 * CHUNK)

        nc.vector.tensor_scalar(out=turns[:, :, 0], in0=pos[:], scalar1=0.5 / math.pi, scalar2=None, op0=ALU.mult)
        ratio = ROPE_BASE ** (-1.0 / (ROT - 1))
        for w in (1, 2, 4, 8, 16):
            nc.vector.tensor_scalar(
                out=turns[:, :, w : 2 * w], in0=turns[:, :, 0:w], scalar1=ratio**w, scalar2=None, op0=ALU.mult
            )
        nc.vector.tensor_copy(out=whole[:], in_=turns[:])
        nc.vector.tensor_tensor(out=frac[:], in0=turns[:], in1=whole[:], op=ALU.subtract)
        nc.scalar.activation(out=sin_t[:, :, 0, :], in_=frac[:], func=ACT.Sin, scale=-2.0 * math.pi)
        nc.scalar.activation(out=sin_t[:, :, 1, :], in_=frac[:], func=ACT.Sin, scale=2.0 * math.pi)
        nc.scalar.activation(out=half_sin[:], in_=frac[:], func=ACT.Sin, scale=math.pi)
        nc.vector.scalar_tensor_tensor(
            out=cos_t[:], in0=half_sin[:], scalar=-2.0, in1=half_sin[:], op0=ALU.mult, op1=ALU.mult
        )
        nc.vector.tensor_scalar(out=cos_t[:], in0=cos_t[:], scalar1=1.0, scalar2=None, op0=ALU.add)

        def bank(i):
            return psum.tile([P, CHUNK], F32, name="bank%d" % (i % 8), tag="bank%d" % (i % 8))

        warm = bank(7)
        for i in range(WARMUPS):
            nc.tensor.matmul(out=warm[:], lhsT=zeros[:, 0:P], rhs=zeros[:], start=True, stop=True)

        def mm(acc, g, b, c, a, n):
            s = max(c - 1, 0)
            o = c * CHUNK - first[s] + a
            nc.tensor.matmul_mx(
                out=acc[:, a : a + n],
                lhsT=xc[:, g, 2 * P * b : 2 * P * (b + 1)].bitcast(FP4X4),
                lhsT_scale=xs[:, g, P * b : P * (b + 1)],
                rhs=wc[s][:, g, 2 * o : 2 * (o + n)].bitcast(FP4X4),
                rhs_scale=ws[s][:, g, o : o + n],
                start=(g == 0),
                stop=(g == PASSES - 1),
            )

        def store(res, b, c, a, n, queue):
            dst, o = outs[c]
            queue.dma_start(out=dst[P * b : P * (b + 1), o + a : o + a + n], in_=res[:, a : a + n])

        def rope(acc, b, c):
            res = work.tile([P, CHUNK], F32, name="res", bufs=24, align_bytes=256)
            t_cos = work.tile([P, 8, ROT], F32, name="t_cos", align_bytes=256)
            t_sin = work.tile([P, 4, 2, ROT], F32, name="t_sin", align_bytes=256)
            src = acc[:].rearrange("p (h s r j) -> p h s r j", h=4, s=2, r=2)
            src8 = acc[:].rearrange("p (h r j) -> p h r j", h=8, r=2)
            dst = res[:].rearrange("p (h s r j) -> p h s r j", h=4, s=2, r=2)
            dst8 = res[:].rearrange("p (h r j) -> p h r j", h=8, r=2)
            nc.vector.tensor_tensor(
                out=t_cos[:],
                in0=src8[:, :, 0, :],
                in1=cos_t[:, b, :].unsqueeze(1).to_broadcast([P, 8, ROT]),
                op=ALU.mult,
            )
            nc.vector.tensor_tensor(
                out=t_sin[:],
                in0=src[:, :, :, 0, :],
                in1=sin_t[:, b, :, :].unsqueeze(1).to_broadcast([P, 4, 2, ROT]),
                op=ALU.mult,
            )
            nc.scalar.copy(out=dst8[:, :, 1, :], in_=src8[:, :, 1, :])
            nc.vector.tensor_tensor(
                out=dst[:, :, :, 0, :],
                in0=t_cos[:].rearrange("p (h s) j -> p h s j", s=2),
                in1=t_sin[:, :, ::-1, :],
                op=ALU.add,
            )
            store(res, b, c, 0, CHUNK, nc.sync)

        accs = [bank(i) for i in range(8)]
        for g in range(PASSES):
            for i in range(8):
                mm(accs[i], g, i % 4, i // 4, 0, CHUNK)
        for i in range(8):
            rope(accs[i], i % 4, i // 4)

        i = 0
        for c in (2, 3, 4, 5):
            for b in range(4):
                last = c == 5 and b == 3
                for a, n in [(0, 256), (256, 128), (384, 128)] if last else [(0, CHUNK)]:
                    acc = bank(i)
                    i += 1
                    for g in range(PASSES):
                        mm(acc, g, b, c, a, n)
                    if c < 5:
                        rope(acc, b, c)
                    else:
                        res = work.tile([P, CHUNK], F32, name="res", bufs=24, align_bytes=256)
                        if a == 256:
                            nc.vector.tensor_copy(out=res[:, a : a + n], in_=acc[:, a : a + n])
                        else:
                            nc.scalar.copy(out=res[:, a : a + n], in_=acc[:, a : a + n])
                        store(res, b, c, a, n, nc.scalar if a == 384 else nc.sync)
